import numpy as np
import ml_dtypes


def mxq(x, axis, fmt="e4m3"):
    dtype, down = {"e4m3": (ml_dtypes.float8_e4m3fn, 7), "e5m2": (ml_dtypes.float8_e5m2, 14)}[fmt]
    v = np.moveaxis(np.asarray(x, np.float32).astype(ml_dtypes.bfloat16).astype(np.float64), axis, -1)
    blocks = v.reshape(v.shape[:-1] + (-1, 32))
    amax = np.abs(blocks).max(-1, keepdims=True)
    byte = np.maximum(np.where(amax > 0, np.frexp(amax)[1] - 1 + 127, 0) - down, 1)
    scale = np.exp2(byte - 127.0)
    codes = (blocks / scale).astype(np.float32).astype(dtype).astype(np.float64)
    return np.moveaxis((codes * scale).reshape(v.shape), -1, axis)


WIDE = False


def mx_kscale(k):
    if not WIDE:
        return np.ones(k)
    levels = np.array([20, -20, 10, -10, 0])
    a = np.random.permutation(np.resize(levels, k // 512 * 4)).reshape(k // 512, 4)
    idx = np.arange(k)
    return np.exp2(a[idx // 512, idx % 128 // 32])


BF16 = ml_dtypes.bfloat16


def bf(x):
    return np.asarray(x, np.float32).astype(BF16)


def f64(x):
    return np.asarray(x).astype(np.float64)


B, S, D, O, G, P = 2, 512, 1024, 512, 3, 3
NB = G + P


def silu(v):
    return v / (1.0 + np.exp(-v))


def dsilu(v):
    sg = 1.0 / (1.0 + np.exp(-v))
    return sg * (1.0 + v * (1.0 - sg))


def extended_grid(d):
    pts = np.linspace(-1.0, 1.0, G + 1)
    h = 2.0 / G
    left = pts[0] + h * np.arange(-P, 0)
    right = pts[-1] + h * np.arange(1, P + 1)
    ext = np.concatenate([left, pts, right])
    return np.broadcast_to(ext, (d, ext.shape[0]))


def bspline(x, grid, order):
    x = x[:, :, None]
    g = grid[None, :, :]
    bb = ((x >= g[..., :-1]) & (x < g[..., 1:])).astype(np.float64)
    for p in range(1, order + 1):
        left = (x - g[..., :-(p + 1)]) / (g[..., p:-1] - g[..., :-(p + 1)])
        right = (g[..., p + 1:] - x) / (g[..., p + 1:] - g[..., 1:-p])
        bb = left * bb[..., :-1] + right * bb[..., 1:]
    return bb


def bspline_dbasis(x, grid):
    lo = bspline(x, grid, P - 1)
    g = grid[None, :, :]
    return P * (lo[..., :-1] / (g[..., P:-1] - g[..., :-(P + 1)]) - lo[..., 1:] / (g[..., P + 1:] - g[..., 1:-P]))


def setup_inputs():
    u = mx_kscale(O)
    x = np.random.standard_normal((B, S, D))
    coef = np.random.standard_normal((O, D, NB)) * 2.0 / np.sqrt(D) / u[:, None, None]
    scale_base = (0.25 + (np.random.uniform(size=(O, D)) * 2.0 - 1.0) * 2.0) / np.sqrt(D) / u[:, None]
    scale_sp = 1.0 + 0.1 * np.random.standard_normal((O, D))
    bias = 0.1 * np.random.standard_normal(O)
    g = np.random.standard_normal((B, S, O)) * np.exp2(np.random.randint(-12, 1, (B, S, 1))) * 4.0 * u
    return {"x": bf(x), "coef": bf(coef), "scale_base": bf(scale_base), "scale_sp": bf(scale_sp), "bias": bf(bias), "grad_out": bf(g)}


def reference(x, coef, scale_base, scale_sp, bias, grad_out):
    x = f64(x)
    b_, s_, d = x.shape
    xf = x.reshape(-1, d)
    g = f64(grad_out)
    o = g.shape[-1]
    gq = mxq(g.reshape(-1, o), 1, "e5m2")
    spline_w = (f64(scale_sp)[..., None] * f64(coef)).reshape(o, d * NB)
    t_base = gq @ mxq(f64(scale_base), 0, "e4m3")
    t_sp = (gq @ mxq(spline_w, 0, "e4m3")).reshape(-1, d, NB)
    db = bspline_dbasis(xf, extended_grid(d))
    gx = dsilu(xf) * t_base + (db * t_sp).sum(-1)
    return gx.reshape(b_, s_, d)

@@ -1,0 +1,194 @@
+from contextlib import ExitStack
+import math
+
+import concourse.mybir as mybir
+from concourse.masks import make_identity
+
+F32 = mybir.dt.float32
+BF16 = mybir.dt.bfloat16
+U32 = mybir.dt.uint32
+U8 = mybir.dt.uint8
+E4X4 = mybir.dt.float8_e4m3fn_x4
+E5X4 = mybir.dt.float8_e5m2_x4
+ALU = mybir.AluOpType
+ACT = mybir.ActivationFunctionType
+
+P = 128
+NBLK = 8
+D = 1024
+O = 512
+NB = 6
+HALF = 512
+CH = 256
+
+FLOPS = 2 * 1024 * 512 * 7168
+
+SUMS = (
+    ("base", ((1, 0),)),
+    ("d03", ((1, 4), (-1, 3), (-1, 1))),
+    ("e0", ((1, 1),)),
+    ("d36", ((-1, 6), (-1, 4), (1, 3))),
+    ("d14", ((1, 5), (-1, 4), (-1, 2), (1, 1))),
+    ("e1", ((1, 2), (-1, 1))),
+    ("d25", ((1, 6), (-1, 5), (-1, 3), (1, 2))),
+    ("e2", ((1, 3), (-1, 2))),
+)
+
+
+def tile_kanoriginal_t_kernel(tc, x, coef, scale_base, scale_sp, bias, grad_out, out):
+    nc = tc.nc
+    xv = x.flatten_outer_dims().rearrange("(p k) d -> p k d", k=NBLK)
+    gv = grad_out.flatten_outer_dims().rearrange("(p k) o -> p k o", k=NBLK)
+    ov = out.flatten_outer_dims().rearrange("(p k) d -> p k d", k=NBLK)
+    cv = coef.rearrange("(p t) i b -> p t (i b)", t=4)
+    spv = scale_sp.rearrange("(p t) i -> p t i", t=4)
+    sbv = scale_base.rearrange("(p t) i -> p t i", t=4)
+
+    with ExitStack() as ctx:
+        keep = ctx.enter_context(tc.tile_pool(name="keep", bufs=1))
+        fac = ctx.enter_context(tc.tile_pool(name="fac", bufs=2))
+        psum = ctx.enter_context(tc.psum_pool(name="psum", bufs=1))
+
+        x_all = keep.tile([P, NBLK, D], BF16)
+        ds_all = keep.tile([P, NBLK, D], F32)
+        wq = keep.tile([P, 7, D], U32, align_bytes=64)
+        ws = keep.tile([P, 7, D], U8, align_bytes=64)
+        gq_pos = keep.tile([P, NBLK * P], U32, align_bytes=64)
+        gs_pos = keep.tile([P, NBLK * P], U8, align_bytes=64)
+        gq_neg = keep.tile([P, NBLK * P], U32, align_bytes=64)
+        gs_neg = keep.tile([P, NBLK * P], U8, align_bytes=64)
+        ident = keep.tile([P, P], F32)
+
+        with tc.tile_pool(name="prep1", bufs=1) as prep1, tc.tile_pool(name="prep2", bufs=2) as prep2:
+            g_raw = prep1.tile([P, NBLK, O], BF16, tag="ga", align_bytes=64)
+            nc.sync.dma_start(out=g_raw[:], in_=gv)
+            sp_raw = prep1.tile([P, 4, D], BF16, tag="sp")
+            nc.sync.dma_start(out=sp_raw[:], in_=spv)
+            craws = []
+            for c in range(2):
+                craw = prep2.tile([P, 4, CH * NB], BF16, name="craw%d" % c, tag="craw")
+                nc.sync.dma_start(out=craw[:], in_=cv[:, :, c * CH * NB:(c + 1) * CH * NB])
+                craws.append(craw)
+                if c == 0:
+                    nc.sync.dma_start(out=x_all[:], in_=xv)
+
+            make_identity(nc, ident[:])
+
+            g_pos = prep1.tile([P, NBLK * P, 4], BF16, tag="gb", align_bytes=64)
+            g_pos32 = g_pos[:].rearrange("p n t -> p (n t)").bitcast(F32).rearrange("p (k n u) -> p k n u", k=NBLK, u=2)
+            names = [s[0] for s in SUMS]
+            for q in range(4):
+                pt = psum.tile([P, 4, P], F32, name="pt%d" % q, tag=names[q])
+                for kl in range(2):
+                    words = g_raw[:, 2 * q + kl, :].bitcast(F32).rearrange("p (w u) -> p u w", u=2)
+                    for u in range(2):
+                        nc.tensor.transpose(pt[:, 2 * kl + u, :], words[:, u, :], ident[:])
+                nc.vector.tensor_copy(
+                    out=g_pos32[:, 2 * q:2 * q + 2],
+                    in_=pt[:].rearrange("p (k u) n -> p k n u", u=2),
+                )
+            g_flat = g_pos[:].rearrange("p n t -> p (n t)")
+            nc.vector.quantize_mx(out=gq_pos[:].bitcast(E5X4), scales=gs_pos[:], in_=g_flat)
+            g_neg = prep1.tile([P, NBLK * P * 4], BF16, tag="gc", align_bytes=64)
+            nc.vector.tensor_scalar(out=g_neg[:], in0=g_flat, scalar1=-1.0, scalar2=None, op0=ALU.mult)
+            nc.vector.quantize_mx(out=gq_neg[:].bitcast(E5X4), scales=gs_neg[:], in_=g_neg[:])
+
+            sb_raw = prep1.tile([P, 4, D], BF16, tag="ga", align_bytes=64)
+            nc.sync.dma_start(out=sb_raw[:], in_=sbv)
+            sb_grp = prep1.tile([P, D, 4], BF16, tag="gb", align_bytes=64)
+            nc.scalar.copy(out=sb_grp[:], in_=sb_raw[:].rearrange("p t i -> p i t"))
+            nc.vector.quantize_mx(out=wq[:, 0, :].bitcast(E4X4), scales=ws[:, 0, :], in_=sb_grp[:].rearrange("p i t -> p (i t)"))
+
+            for c in range(4):
+                if c < 2:
+                    craw = craws[c]
+                else:
+                    craw = prep2.tile([P, 4, CH * NB], BF16, name="craw%d" % c, tag="craw")
+                    nc.sync.dma_start(out=craw[:], in_=cv[:, :, c * CH * NB:(c + 1) * CH * NB])
+                cols = slice(c * CH, (c + 1) * CH)
+                cview = craw[:].rearrange("p t (i b) -> p b i t", b=NB)
+                sview = sp_raw[:, :, cols].rearrange("p t i -> p i t").unsqueeze(1).to_broadcast([P, 3, CH, 4])
+                for hb in range(2):
+                    gw = prep2.tile([P, 3, CH, 4], BF16, name="gw", tag="gw", align_bytes=64)
+                    nc.vector.tensor_tensor(out=gw[:], in0=cview[:, 3 * hb:3 * hb + 3], in1=sview, op=ALU.mult)
+                    for j in range(3):
+                        term = 1 + 3 * hb + j
+                        nc.vector.quantize_mx(
+                            out=wq[:, term, cols].bitcast(E4X4),
+                            scales=ws[:, term, cols],
+                            in_=gw[:, j].rearrange("p i t -> p (i t)"),
+                        )
+
+        for k in range(4):
+            xs = x_all[:, 2 * k:2 * k + 2, :]
+            dsl = ds_all[:, 2 * k:2 * k + 2, :]
+            nc.scalar.activation(out=dsl, in_=xs, func=ACT.Sigmoid)
+            sn = fac.tile([P, 3, D], F32, name="sn", tag="w")
+            nc.scalar.activation(out=sn[:, 0:2, :], in_=xs, func=ACT.Sigmoid, scale=-1.0)
+            nc.gpsimd.tensor_tensor(out=sn[:, 0:2, :], in0=xs, in1=sn[:, 0:2, :], op=ALU.mult)
+            nc.vector.scalar_tensor_tensor(out=dsl, in0=sn[:, 0:2, :], scalar=1.0, in1=dsl, op0=ALU.add, op1=ALU.mult)
+
+        def factors(k):
+            xk = x_all[:, k, :]
+            xc0 = fac.tile([P, D], BF16, name="xc0", tag="xc0")
+            nc.vector.tensor_scalar(out=xc0[:], in0=xk, scalar1=3.0, scalar2=-3.0, op0=ALU.min, op1=ALU.max)
+            w = fac.tile([P, 3, D], F32, name="w", tag="w")
+            nc.vector.tensor_scalar(out=w[:, 1, :], in0=xk, scalar1=5.0 / 3.0, scalar2=-7.0 / 3.0, op0=ALU.min, op1=ALU.max)
+            nc.vector.tensor_scalar(out=w[:, 2, :], in0=xk, scalar1=7.0 / 3.0, scalar2=-5.0 / 3.0, op0=ALU.min, op1=ALU.max)
+            nc.scalar.activation(out=w[:, 0, :], in_=xc0[:], func=ACT.Abs, scale=1.5)
+            nc.scalar.activation(out=w[:, 0, :], in_=w[:, 0, :], func=ACT.Abs, bias=-1.5)
+            nc.scalar.activation(out=w[:, 1, :], in_=w[:, 1, :], func=ACT.Abs, scale=1.5, bias=0.5)
+            nc.scalar.activation(out=w[:, 2, :], in_=w[:, 2, :], func=ACT.Abs, scale=1.5, bias=-0.5)
+            nc.scalar.activation(out=w[:], in_=w[:], func=ACT.Abs, bias=-1.5)
+            f = fac.tile([P, 3, D], F32, name="f", tag="f")
+            r = math.sqrt(0.75)
+            nc.scalar.activation(out=f[:], in_=w[:], func=ACT.Square, scale=-r, bias=1.5 * r)
+            nc.scalar.activation(out=w[:], in_=w[:], func=ACT.Relu, scale=-1.0, bias=0.5)
+            nc.scalar.activation(out=w[:], in_=w[:], func=ACT.Square, scale=1.5)
+            nc.gpsimd.tensor_tensor(out=f[:], in0=f[:], in1=w[:], op=ALU.subtract)
+            return f
+
+        with tc.tile_pool(name="tside", bufs=2) as tp:
+            f_next = factors(0)
+            for k in range(NBLK):
+                f = f_next
+                if k + 1 < NBLK:
+                    f_next = factors(k + 1)
+                tok = slice(k * P, (k + 1) * P)
+                for ic in range(2):
+                    cols = slice(ic * HALF, (ic + 1) * HALF)
+                    ps = {}
+                    for name, passes in SUMS:
+                        acc = psum.tile([P, HALF], F32, name="ps_" + name, tag=name)
+                        ps[name] = acc
+                        for j, (sign, term) in enumerate(passes):
+                            gq = gq_pos if sign > 0 else gq_neg
+                            gs = gs_pos if sign > 0 else gs_neg
+                            nc.tensor.matmul_mx(
+                                out=acc[:],
+                                lhsT=gq[:, tok].bitcast(E5X4),
+                                lhsT_scale=gs[:, tok],
+                                rhs=wq[:, term, cols].bitcast(E4X4),
+                                rhs_scale=ws[:, term, cols],
+                                start=(j == 0),
+                                stop=(j == len(passes) - 1),
+                            )
+                    xk = x_all[:, k, cols]
+                    prod = tp.tile([P, 4, HALF], F32, name="prod", tag="prod")
+                    sel = tp.tile([P, 3, HALF], F32, name="sel", tag="sel")
+                    t36 = tp.tile([P, HALF], F32, name="t36", tag="t36")
+                    nc.vector.tensor_tensor(out=prod[:, 3, :], in0=ds_all[:, k, cols], in1=ps["base"][:], op=ALU.mult)
+                    nc.vector.scalar_tensor_tensor(out=sel[:, 0, :], in0=xk, scalar=-1.0, in1=ps["d03"][:], op0=ALU.is_ge, op1=ALU.mult)
+                    nc.vector.tensor_tensor(out=sel[:, 0, :], in0=sel[:, 0, :], in1=ps["e0"][:], op=ALU.add)
+                    nc.vector.scalar_tensor_tensor(out=t36[:], in0=xk, scalar=1.0, in1=ps["d36"][:], op0=ALU.is_ge, op1=ALU.mult)
+                    nc.vector.tensor_tensor(out=sel[:, 0, :], in0=sel[:, 0, :], in1=t36[:], op=ALU.add)
+                    nc.vector.scalar_tensor_tensor(out=sel[:, 1, :], in0=xk, scalar=-1.0 / 3.0, in1=ps["d14"][:], op0=ALU.is_ge, op1=ALU.mult)
+                    nc.vector.tensor_tensor(out=sel[:, 1, :], in0=sel[:, 1, :], in1=ps["e1"][:], op=ALU.add)
+                    nc.vector.scalar_tensor_tensor(out=sel[:, 2, :], in0=xk, scalar=1.0 / 3.0, in1=ps["d25"][:], op0=ALU.is_ge, op1=ALU.mult)
+                    nc.vector.tensor_tensor(out=sel[:, 2, :], in0=sel[:, 2, :], in1=ps["e2"][:], op=ALU.add)
+                    nc.vector.tensor_tensor(out=prod[:, 0:3, :], in0=sel[:], in1=f[:, :, cols], op=ALU.mult)
+                    half = tp.tile([P, 2, HALF], F32, name="half", tag="half")
+                    nc.gpsimd.tensor_tensor(out=half[:], in0=prod[:, 0:2, :], in1=prod[:, 2:4, :], op=ALU.add)
+                    res = tp.tile([P, HALF], F32, name="res", tag="res")
+                    nc.gpsimd.tensor_tensor(out=res[:], in0=half[:, 0, :], in1=half[:, 1, :], op=ALU.add)
+                    nc.sync.dma_start(out=ov[:, k, cols], in_=res[:])

@@ -20,11 +20,16 @@ O = 512
 NB = 6
 HALF = 512
 CH = 256
+NT = 16
+AHEAD = 3
+PIN = False
+SUB_ON_G = True
+CLAMP_ON_G = True
 
 FLOPS = 2 * 1024 * 512 * 7168
 
 SUMS = (
-    ("base", ((1, 0),)),
+    ("base", ((-1, 0),)),
     ("d03", ((1, 4), (-1, 3), (-1, 1))),
     ("e0", ((1, 1),)),
     ("d36", ((-1, 6), (-1, 4), (1, 3))),
@@ -45,8 +50,11 @@ def tile_kanoriginal_t_kernel(tc, x, coef, scale_base, scale_sp, bias, grad_out,
     sbv = scale_base.rearrange("(p t) i -> p t i", t=4)
 
     with ExitStack() as ctx:
+        if PIN:
+            ctx.enter_context(tc.manual_schedule())
         keep = ctx.enter_context(tc.tile_pool(name="keep", bufs=1))
-        fac = ctx.enter_context(tc.tile_pool(name="fac", bufs=2))
+        facw = ctx.enter_context(tc.tile_pool(name="facw", bufs=3))
+        facf = ctx.enter_context(tc.tile_pool(name="facf", bufs=AHEAD + 2))
         psum = ctx.enter_context(tc.psum_pool(name="psum", bufs=1))
 
         x_all = keep.tile([P, NBLK, D], BF16)
@@ -88,16 +96,15 @@ def tile_kanoriginal_t_kernel(tc, x, coef, scale_base, scale_sp, bias, grad_out,
                     in_=pt[:].rearrange("p (k u) n -> p k n u", u=2),
                 )
             g_flat = g_pos[:].rearrange("p n t -> p (n t)")
-            nc.vector.quantize_mx(out=gq_pos[:].bitcast(E5X4), scales=gs_pos[:], in_=g_flat)
             g_neg = prep1.tile([P, NBLK * P * 4], BF16, tag="gc", align_bytes=64)
             nc.vector.tensor_scalar(out=g_neg[:], in0=g_flat, scalar1=-1.0, scalar2=None, op0=ALU.mult)
+            nc.vector.quantize_mx(out=gq_pos[:].bitcast(E5X4), scales=gs_pos[:], in_=g_flat)
             nc.vector.quantize_mx(out=gq_neg[:].bitcast(E5X4), scales=gs_neg[:], in_=g_neg[:])
 
             sb_raw = prep1.tile([P, 4, D], BF16, tag="ga", align_bytes=64)
             nc.sync.dma_start(out=sb_raw[:], in_=sbv)
             sb_grp = prep1.tile([P, D, 4], BF16, tag="gb", align_bytes=64)
             nc.scalar.copy(out=sb_grp[:], in_=sb_raw[:].rearrange("p t i -> p i t"))
-            nc.vector.quantize_mx(out=wq[:, 0, :].bitcast(E4X4), scales=ws[:, 0, :], in_=sb_grp[:].rearrange("p i t -> p (i t)"))
 
             for c in range(4):
                 if c < 2:
@@ -108,87 +115,106 @@ def tile_kanoriginal_t_kernel(tc, x, coef, scale_base, scale_sp, bias, grad_out,
                 cols = slice(c * CH, (c + 1) * CH)
                 cview = craw[:].rearrange("p t (i b) -> p b i t", b=NB)
                 sview = sp_raw[:, :, cols].rearrange("p t i -> p i t").unsqueeze(1).to_broadcast([P, 3, CH, 4])
+                gws = []
                 for hb in range(2):
-                    gw = prep2.tile([P, 3, CH, 4], BF16, name="gw", tag="gw", align_bytes=64)
+                    gw = prep2.tile([P, 3, CH, 4], BF16, name="gw%d" % hb, tag="gw", align_bytes=64)
                     nc.vector.tensor_tensor(out=gw[:], in0=cview[:, 3 * hb:3 * hb + 3], in1=sview, op=ALU.mult)
+                    gws.append(gw)
+                for hb in range(2):
                     for j in range(3):
                         term = 1 + 3 * hb + j
                         nc.vector.quantize_mx(
                             out=wq[:, term, cols].bitcast(E4X4),
                             scales=ws[:, term, cols],
-                            in_=gw[:, j].rearrange("p i t -> p (i t)"),
+                            in_=gws[hb][:, j].rearrange("p i t -> p (i t)"),
                         )
+                if c == 0:
+                    nc.vector.quantize_mx(out=wq[:, 0, :].bitcast(E4X4), scales=ws[:, 0, :], in_=sb_grp[:].rearrange("p i t -> p (i t)"))
 
-        for k in range(4):
-            xs = x_all[:, 2 * k:2 * k + 2, :]
-            dsl = ds_all[:, 2 * k:2 * k + 2, :]
-            nc.scalar.activation(out=dsl, in_=xs, func=ACT.Sigmoid)
-            sn = fac.tile([P, 3, D], F32, name="sn", tag="w")
-            nc.scalar.activation(out=sn[:, 0:2, :], in_=xs, func=ACT.Sigmoid, scale=-1.0)
-            nc.gpsimd.tensor_tensor(out=sn[:, 0:2, :], in0=xs, in1=sn[:, 0:2, :], op=ALU.mult)
-            nc.vector.scalar_tensor_tensor(out=dsl, in0=sn[:, 0:2, :], scalar=1.0, in1=dsl, op0=ALU.add, op1=ALU.mult)
+            for k in range(NBLK):
+                nc.scalar.activation(out=ds_all[:, k, :], in_=x_all[:, k, :], func=ACT.Silu, scale=-1.0)
+            for k in range(NBLK):
+                sg = prep2.tile([P, D], F32, name="sg", tag="sg")
+                nc.scalar.activation(out=sg[:], in_=x_all[:, k, :], func=ACT.Sigmoid)
+                nc.vector.scalar_tensor_tensor(out=ds_all[:, k, :], in0=ds_all[:, k, :], scalar=1.0, in1=sg[:], op0=ALU.subtract, op1=ALU.mult)
 
-        def factors(k):
-            xk = x_all[:, k, :]
-            xc0 = fac.tile([P, D], BF16, name="xc0", tag="xc0")
+        wtiles = {}
+        ftiles = {}
+
+        def xslice(i):
+            return x_all[:, i // 2, (i % 2) * HALF:(i % 2 + 1) * HALF]
+
+        def clamps(i):
+            xk = xslice(i)
+            xc0 = facw.tile([P, HALF], BF16, name="xc0", tag="xc0")
             nc.vector.tensor_scalar(out=xc0[:], in0=xk, scalar1=3.0, scalar2=-3.0, op0=ALU.min, op1=ALU.max)
-            w = fac.tile([P, 3, D], F32, name="w", tag="w")
-            nc.vector.tensor_scalar(out=w[:, 1, :], in0=xk, scalar1=5.0 / 3.0, scalar2=-7.0 / 3.0, op0=ALU.min, op1=ALU.max)
-            nc.vector.tensor_scalar(out=w[:, 2, :], in0=xk, scalar1=7.0 / 3.0, scalar2=-5.0 / 3.0, op0=ALU.min, op1=ALU.max)
+            w = facw.tile([P, 3, HALF], F32, name="w", tag="w")
+            eng = nc.gpsimd if CLAMP_ON_G else nc.vector
+            eng.tensor_scalar(out=w[:, 1, :], in0=xk, scalar1=5.0 / 3.0, scalar2=-7.0 / 3.0, op0=ALU.min, op1=ALU.max)
+            eng.tensor_scalar(out=w[:, 2, :], in0=xk, scalar1=7.0 / 3.0, scalar2=-5.0 / 3.0, op0=ALU.min, op1=ALU.max)
+            wtiles[i] = (xc0, w)
+
+        def factor(i):
+            if i + 1 < NT:
+                clamps(i + 1)
+            xc0, w = wtiles[i]
             nc.scalar.activation(out=w[:, 0, :], in_=xc0[:], func=ACT.Abs, scale=1.5)
             nc.scalar.activation(out=w[:, 0, :], in_=w[:, 0, :], func=ACT.Abs, bias=-1.5)
             nc.scalar.activation(out=w[:, 1, :], in_=w[:, 1, :], func=ACT.Abs, scale=1.5, bias=0.5)
             nc.scalar.activation(out=w[:, 2, :], in_=w[:, 2, :], func=ACT.Abs, scale=1.5, bias=-0.5)
             nc.scalar.activation(out=w[:], in_=w[:], func=ACT.Abs, bias=-1.5)
-            f = fac.tile([P, 3, D], F32, name="f", tag="f")
+            f = facf.tile([P, 3, HALF], F32, name="f", tag="f")
             r = math.sqrt(0.75)
             nc.scalar.activation(out=f[:], in_=w[:], func=ACT.Square, scale=-r, bias=1.5 * r)
             nc.scalar.activation(out=w[:], in_=w[:], func=ACT.Relu, scale=-1.0, bias=0.5)
             nc.scalar.activation(out=w[:], in_=w[:], func=ACT.Square, scale=1.5)
-            nc.gpsimd.tensor_tensor(out=f[:], in0=f[:], in1=w[:], op=ALU.subtract)
-            return f
+            eng = nc.gpsimd if SUB_ON_G else nc.vector
+            eng.tensor_tensor(out=f[:], in0=f[:], in1=w[:], op=ALU.subtract)
+            ftiles[i] = f
 
-        with tc.tile_pool(name="tside", bufs=2) as tp:
-            f_next = factors(0)
-            for k in range(NBLK):
-                f = f_next
-                if k + 1 < NBLK:
-                    f_next = factors(k + 1)
+        with tc.tile_pool(name="tside", bufs=3) as tp:
+            clamps(0)
+            for i in range(AHEAD):
+                factor(i)
+            for i in range(NT):
+                if i + AHEAD < NT:
+                    factor(i + AHEAD)
+                k = i // 2
+                f = ftiles[i]
                 tok = slice(k * P, (k + 1) * P)
-                for ic in range(2):
-                    cols = slice(ic * HALF, (ic + 1) * HALF)
-                    ps = {}
-                    for name, passes in SUMS:
-                        acc = psum.tile([P, HALF], F32, name="ps_" + name, tag=name)
-                        ps[name] = acc
-                        for j, (sign, term) in enumerate(passes):
-                            gq = gq_pos if sign > 0 else gq_neg
-                            gs = gs_pos if sign > 0 else gs_neg
-                            nc.tensor.matmul_mx(
-                                out=acc[:],
-                                lhsT=gq[:, tok].bitcast(E5X4),
-                                lhsT_scale=gs[:, tok],
-                                rhs=wq[:, term, cols].bitcast(E4X4),
-                                rhs_scale=ws[:, term, cols],
-                                start=(j == 0),
-                                stop=(j == len(passes) - 1),
-                            )
-                    xk = x_all[:, k, cols]
-                    prod = tp.tile([P, 4, HALF], F32, name="prod", tag="prod")
-                    sel = tp.tile([P, 3, HALF], F32, name="sel", tag="sel")
-                    t36 = tp.tile([P, HALF], F32, name="t36", tag="t36")
-                    nc.vector.tensor_tensor(out=prod[:, 3, :], in0=ds_all[:, k, cols], in1=ps["base"][:], op=ALU.mult)
-                    nc.vector.scalar_tensor_tensor(out=sel[:, 0, :], in0=xk, scalar=-1.0, in1=ps["d03"][:], op0=ALU.is_ge, op1=ALU.mult)
-                    nc.vector.tensor_tensor(out=sel[:, 0, :], in0=sel[:, 0, :], in1=ps["e0"][:], op=ALU.add)
-                    nc.vector.scalar_tensor_tensor(out=t36[:], in0=xk, scalar=1.0, in1=ps["d36"][:], op0=ALU.is_ge, op1=ALU.mult)
-                    nc.vector.tensor_tensor(out=sel[:, 0, :], in0=sel[:, 0, :], in1=t36[:], op=ALU.add)
-                    nc.vector.scalar_tensor_tensor(out=sel[:, 1, :], in0=xk, scalar=-1.0 / 3.0, in1=ps["d14"][:], op0=ALU.is_ge, op1=ALU.mult)
-                    nc.vector.tensor_tensor(out=sel[:, 1, :], in0=sel[:, 1, :], in1=ps["e1"][:], op=ALU.add)
-                    nc.vector.scalar_tensor_tensor(out=sel[:, 2, :], in0=xk, scalar=1.0 / 3.0, in1=ps["d25"][:], op0=ALU.is_ge, op1=ALU.mult)
-                    nc.vector.tensor_tensor(out=sel[:, 2, :], in0=sel[:, 2, :], in1=ps["e2"][:], op=ALU.add)
-                    nc.vector.tensor_tensor(out=prod[:, 0:3, :], in0=sel[:], in1=f[:, :, cols], op=ALU.mult)
-                    half = tp.tile([P, 2, HALF], F32, name="half", tag="half")
-                    nc.gpsimd.tensor_tensor(out=half[:], in0=prod[:, 0:2, :], in1=prod[:, 2:4, :], op=ALU.add)
-                    res = tp.tile([P, HALF], F32, name="res", tag="res")
-                    nc.gpsimd.tensor_tensor(out=res[:], in0=half[:, 0, :], in1=half[:, 1, :], op=ALU.add)
-                    nc.sync.dma_start(out=ov[:, k, cols], in_=res[:])
+                cols = slice((i % 2) * HALF, (i % 2 + 1) * HALF)
+                ps = {}
+                for name, passes in SUMS:
+                    acc = psum.tile([P, HALF], F32, name="ps_" + name, tag=name)
+                    ps[name] = acc
+                    for j, (sign, term) in enumerate(passes):
+                        gq = gq_pos if sign > 0 else gq_neg
+                        gs = gs_pos if sign > 0 else gs_neg
+                        nc.tensor.matmul_mx(
+                            out=acc[:],
+                            lhsT=gq[:, tok].bitcast(E5X4),
+                            lhsT_scale=gs[:, tok],
+                            rhs=wq[:, term, cols].bitcast(E4X4),
+                            rhs_scale=ws[:, term, cols],
+                            start=(j == 0),
+                            stop=(j == len(passes) - 1),
+                        )
+                xk = xslice(i)
+                prod = tp.tile([P, 4, HALF], F32, name="prod", tag="prod")
+                sel = tp.tile([P, 3, HALF], F32, name="sel", tag="sel")
+                t36 = tp.tile([P, HALF], F32, name="t36", tag="t36")
+                nc.vector.tensor_tensor(out=prod[:, 3, :], in0=ds_all[:, k, cols], in1=ps["base"][:], op=ALU.mult)
+                nc.vector.scalar_tensor_tensor(out=sel[:, 0, :], in0=xk, scalar=-1.0, in1=ps["d03"][:], op0=ALU.is_ge, op1=ALU.mult)
+                nc.vector.tensor_tensor(out=sel[:, 0, :], in0=sel[:, 0, :], in1=ps["e0"][:], op=ALU.add)
+                nc.vector.scalar_tensor_tensor(out=t36[:], in0=xk, scalar=1.0, in1=ps["d36"][:], op0=ALU.is_ge, op1=ALU.mult)
+                nc.vector.scalar_tensor_tensor(out=sel[:, 1, :], in0=xk, scalar=-1.0 / 3.0, in1=ps["d14"][:], op0=ALU.is_ge, op1=ALU.mult)
+                nc.vector.tensor_tensor(out=sel[:, 1, :], in0=sel[:, 1, :], in1=ps["e1"][:], op=ALU.add)
+                nc.vector.scalar_tensor_tensor(out=sel[:, 2, :], in0=xk, scalar=1.0 / 3.0, in1=ps["d25"][:], op0=ALU.is_ge, op1=ALU.mult)
+                nc.vector.tensor_tensor(out=sel[:, 2, :], in0=sel[:, 2, :], in1=ps["e2"][:], op=ALU.add)
+                nc.vector.tensor_tensor(out=sel[:, 0, :], in0=sel[:, 0, :], in1=t36[:], op=ALU.add)
+                nc.vector.tensor_tensor(out=prod[:, 0:3, :], in0=sel[:], in1=f[:], op=ALU.mult)
+                half = tp.tile([P, 2, HALF], F32, name="half", tag="half")
+                nc.vector.tensor_tensor(out=half[:], in0=prod[:, 0:2, :], in1=prod[:, 2:4, :], op=ALU.add)
+                res = tp.tile([P, HALF], F32, name="res", tag="res")
+                nc.vector.tensor_tensor(out=res[:], in0=half[:, 0, :], in1=half[:, 1, :], op=ALU.add)
+                nc.sync.dma_start(out=ov[:, k, cols], in_=res[:])

@@ -24,19 +24,20 @@ NT = 16
 AHEAD = 3
 PIN = False
 SUB_ON_G = True
-CLAMP_ON_G = True
+CLAMP_ON_G = False
+S_CHUNKS = (0,)
 
 FLOPS = 2 * 1024 * 512 * 7168
 
 SUMS = (
-    ("base", ((-1, 0),)),
     ("d03", ((1, 4), (-1, 3), (-1, 1))),
-    ("e0", ((1, 1),)),
-    ("d36", ((-1, 6), (-1, 4), (1, 3))),
     ("d14", ((1, 5), (-1, 4), (-1, 2), (1, 1))),
-    ("e1", ((1, 2), (-1, 1))),
     ("d25", ((1, 6), (-1, 5), (-1, 3), (1, 2))),
+    ("d36", ((-1, 6), (-1, 4), (1, 3))),
+    ("e0", ((1, 1),)),
+    ("e1", ((1, 2), (-1, 1))),
     ("e2", ((1, 3), (-1, 2))),
+    ("base", ((-1, 0),)),
 )
 
 
@@ -48,6 +49,7 @@ def tile_kanoriginal_t_kernel(tc, x, coef, scale_base, scale_sp, bias, grad_out,
     cv = coef.rearrange("(p t) i b -> p t (i b)", t=4)
     spv = scale_sp.rearrange("(p t) i -> p t i", t=4)
     sbv = scale_base.rearrange("(p t) i -> p t i", t=4)
+    CW = CH * NB
 
     with ExitStack() as ctx:
         if PIN:
@@ -67,6 +69,9 @@ def tile_kanoriginal_t_kernel(tc, x, coef, scale_base, scale_sp, bias, grad_out,
         gs_neg = keep.tile([P, NBLK * P], U8, align_bytes=64)
         ident = keep.tile([P, P], F32)
 
+        def regroup(eng_copy, dst, src):
+            eng_copy(out=dst.rearrange("p (c i) t -> p c t i", i=4), in_=src.rearrange("p t (c i) -> p c t i", i=4))
+
         with tc.tile_pool(name="prep1", bufs=1) as prep1, tc.tile_pool(name="prep2", bufs=2) as prep2:
             g_raw = prep1.tile([P, NBLK, O], BF16, tag="ga", align_bytes=64)
             nc.sync.dma_start(out=g_raw[:], in_=gv)
@@ -74,11 +79,10 @@ def tile_kanoriginal_t_kernel(tc, x, coef, scale_base, scale_sp, bias, grad_out,
             nc.sync.dma_start(out=sp_raw[:], in_=spv)
             craws = []
             for c in range(2):
-                craw = prep2.tile([P, 4, CH * NB], BF16, name="craw%d" % c, tag="craw")
-                nc.sync.dma_start(out=craw[:], in_=cv[:, :, c * CH * NB:(c + 1) * CH * NB])
+                craw = prep2.tile([P, 4, CW], BF16, name="craw%d" % c, tag="craw")
+                nc.sync.dma_start(out=craw[:], in_=cv[:, :, c * CW:(c + 1) * CW])
                 craws.append(craw)
-                if c == 0:
-                    nc.sync.dma_start(out=x_all[:], in_=xv)
+            nc.sync.dma_start(out=x_all[:], in_=xv)
 
             make_identity(nc, ident[:])
 
@@ -96,25 +100,29 @@ def tile_kanoriginal_t_kernel(tc, x, coef, scale_base, scale_sp, bias, grad_out,
                     in_=pt[:].rearrange("p (k u) n -> p k n u", u=2),
                 )
             g_flat = g_pos[:].rearrange("p n t -> p (n t)")
-            g_neg = prep1.tile([P, NBLK * P * 4], BF16, tag="gc", align_bytes=64)
-            nc.vector.tensor_scalar(out=g_neg[:], in0=g_flat, scalar1=-1.0, scalar2=None, op0=ALU.mult)
+            spg = prep1.tile([P, D, 4], BF16, tag="ga", align_bytes=64)
+            regroup(nc.vector.tensor_copy, spg[:], sp_raw[:])
             nc.vector.quantize_mx(out=gq_pos[:].bitcast(E5X4), scales=gs_pos[:], in_=g_flat)
-            nc.vector.quantize_mx(out=gq_neg[:].bitcast(E5X4), scales=gs_neg[:], in_=g_neg[:])
+            nc.vector.tensor_scalar(out=g_flat, in0=g_flat, scalar1=-1.0, scalar2=None, op0=ALU.mult)
 
-            sb_raw = prep1.tile([P, 4, D], BF16, tag="ga", align_bytes=64)
+            sb_raw = prep1.tile([P, 4, D], BF16, tag="sp")
             nc.sync.dma_start(out=sb_raw[:], in_=sbv)
-            sb_grp = prep1.tile([P, D, 4], BF16, tag="gb", align_bytes=64)
-            nc.scalar.copy(out=sb_grp[:], in_=sb_raw[:].rearrange("p t i -> p i t"))
 
+            neg_done = False
             for c in range(4):
                 if c < 2:
                     craw = craws[c]
                 else:
-                    craw = prep2.tile([P, 4, CH * NB], BF16, name="craw%d" % c, tag="craw")
-                    nc.sync.dma_start(out=craw[:], in_=cv[:, :, c * CH * NB:(c + 1) * CH * NB])
+                    craw = prep2.tile([P, 4, CW], BF16, name="craw%d" % c, tag="craw")
+                    nc.sync.dma_start(out=craw[:], in_=cv[:, :, c * CW:(c + 1) * CW])
                 cols = slice(c * CH, (c + 1) * CH)
-                cview = craw[:].rearrange("p t (i b) -> p b i t", b=NB)
-                sview = sp_raw[:, :, cols].rearrange("p t i -> p i t").unsqueeze(1).to_broadcast([P, 3, CH, 4])
+                cg = prep2.tile([P, CW, 4], BF16, name="cg", tag="cg")
+                regroup(nc.scalar.copy if c in S_CHUNKS else nc.vector.tensor_copy, cg[:], craw[:])
+                if not neg_done:
+                    nc.vector.quantize_mx(out=gq_neg[:].bitcast(E5X4), scales=gs_neg[:], in_=g_flat)
+                    neg_done = True
+                cview = cg[:].rearrange("p (i b) t -> p b i t", b=NB)
+                sview = spg[:, cols, :].unsqueeze(1).to_broadcast([P, 3, CH, 4])
                 gws = []
                 for hb in range(2):
                     gw = prep2.tile([P, 3, CH, 4], BF16, name="gw%d" % hb, tag="gw", align_bytes=64)
@@ -128,15 +136,19 @@ def tile_kanoriginal_t_kernel(tc, x, coef, scale_base, scale_sp, bias, grad_out,
                             scales=ws[:, term, cols],
                             in_=gws[hb][:, j].rearrange("p i t -> p (i t)"),
                         )
-                if c == 0:
+                if c == 1:
+                    sb_grp = prep1.tile([P, D, 4], BF16, tag="gb", align_bytes=64)
+                    regroup(nc.scalar.copy, sb_grp[:], sb_raw[:])
+                if c == 2:
                     nc.vector.quantize_mx(out=wq[:, 0, :].bitcast(E4X4), scales=ws[:, 0, :], in_=sb_grp[:].rearrange("p i t -> p (i t)"))
 
-            for k in range(NBLK):
-                nc.scalar.activation(out=ds_all[:, k, :], in_=x_all[:, k, :], func=ACT.Silu, scale=-1.0)
-            for k in range(NBLK):
-                sg = prep2.tile([P, D], F32, name="sg", tag="sg")
-                nc.scalar.activation(out=sg[:], in_=x_all[:, k, :], func=ACT.Sigmoid)
-                nc.vector.scalar_tensor_tensor(out=ds_all[:, k, :], in0=ds_all[:, k, :], scalar=1.0, in1=sg[:], op0=ALU.subtract, op1=ALU.mult)
+        for k in range(NBLK):
+            nc.scalar.activation(out=ds_all[:, k, :], in_=x_all[:, k, :], func=ACT.Silu, scale=-1.0)
+        for k in range(NBLK):
+            sgt = facw.tile([P, 3, HALF], F32, name="sgt", tag="w")
+            sg = sgt[:].rearrange("p a b -> p (a b)")[:, 0:D]
+            nc.scalar.activation(out=sg, in_=x_all[:, k, :], func=ACT.Sigmoid)
+            nc.vector.scalar_tensor_tensor(out=ds_all[:, k, :], in0=ds_all[:, k, :], scalar=1.0, in1=sg, op0=ALU.subtract, op1=ALU.mult)
 
         wtiles = {}
         ftiles = {}
@@ -172,49 +184,57 @@ def tile_kanoriginal_t_kernel(tc, x, coef, scale_base, scale_sp, bias, grad_out,
             eng.tensor_tensor(out=f[:], in0=f[:], in1=w[:], op=ALU.subtract)
             ftiles[i] = f
 
-        with tc.tile_pool(name="tside", bufs=3) as tp:
+        def sums_and_select(tp, i):
+            k = i // 2
+            tok = slice(k * P, (k + 1) * P)
+            cols = slice((i % 2) * HALF, (i % 2 + 1) * HALF)
+            ps = {}
+            for name, passes in SUMS:
+                acc = psum.tile([P, HALF], F32, name="ps_" + name, tag=name)
+                ps[name] = acc
+                for j, (sign, term) in enumerate(passes):
+                    gq = gq_pos if sign > 0 else gq_neg
+                    gs = gs_pos if sign > 0 else gs_neg
+                    nc.tensor.matmul_mx(
+                        out=acc[:],
+                        lhsT=gq[:, tok].bitcast(E5X4),
+                        lhsT_scale=gs[:, tok],
+                        rhs=wq[:, term, cols].bitcast(E4X4),
+                        rhs_scale=ws[:, term, cols],
+                        start=(j == 0),
+                        stop=(j == len(passes) - 1),
+                    )
+            xk = xslice(i)
+            sel = tp.tile([P, 4, HALF], F32, name="sel", tag="sel")
+            t36 = tp.tile([P, HALF], F32, name="t36", tag="t36")
+            stt = nc.vector.scalar_tensor_tensor
+            stt(out=sel[:, 0, :], in0=xk, scalar=-1.0, in1=ps["d03"][:], op0=ALU.is_ge, op1=ALU.mult)
+            stt(out=sel[:, 1, :], in0=xk, scalar=-1.0 / 3.0, in1=ps["d14"][:], op0=ALU.is_ge, op1=ALU.mult)
+            stt(out=sel[:, 2, :], in0=xk, scalar=1.0 / 3.0, in1=ps["d25"][:], op0=ALU.is_ge, op1=ALU.mult)
+            stt(out=t36[:], in0=xk, scalar=1.0, in1=ps["d36"][:], op0=ALU.is_ge, op1=ALU.mult)
+            for r in range(3):
+                nc.vector.tensor_tensor(out=sel[:, r, :], in0=sel[:, r, :], in1=ps["e%d" % r][:], op=ALU.add)
+            nc.vector.tensor_tensor(out=sel[:, 3, :], in0=ds_all[:, k, cols], in1=ps["base"][:], op=ALU.mult)
+            return sel, t36
+
+        with tc.tile_pool(name="tside", bufs=4) as tp:
             clamps(0)
             for i in range(AHEAD):
                 factor(i)
-            for i in range(NT):
-                if i + AHEAD < NT:
-                    factor(i + AHEAD)
-                k = i // 2
-                f = ftiles[i]
-                tok = slice(k * P, (k + 1) * P)
-                cols = slice((i % 2) * HALF, (i % 2 + 1) * HALF)
-                ps = {}
-                for name, passes in SUMS:
-                    acc = psum.tile([P, HALF], F32, name="ps_" + name, tag=name)
-                    ps[name] = acc
-                    for j, (sign, term) in enumerate(passes):
-                        gq = gq_pos if sign > 0 else gq_neg
-                        gs = gs_pos if sign > 0 else gs_neg
-                        nc.tensor.matmul_mx(
-                            out=acc[:],
-                            lhsT=gq[:, tok].bitcast(E5X4),
-                            lhsT_scale=gs[:, tok],
-                            rhs=wq[:, term, cols].bitcast(E4X4),
-                            rhs_scale=ws[:, term, cols],
-                            start=(j == 0),
-                            stop=(j == len(passes) - 1),
-                        )
-                xk = xslice(i)
-                prod = tp.tile([P, 4, HALF], F32, name="prod", tag="prod")
-                sel = tp.tile([P, 3, HALF], F32, name="sel", tag="sel")
-                t36 = tp.tile([P, HALF], F32, name="t36", tag="t36")
-                nc.vector.tensor_tensor(out=prod[:, 3, :], in0=ds_all[:, k, cols], in1=ps["base"][:], op=ALU.mult)
-                nc.vector.scalar_tensor_tensor(out=sel[:, 0, :], in0=xk, scalar=-1.0, in1=ps["d03"][:], op0=ALU.is_ge, op1=ALU.mult)
-                nc.vector.tensor_tensor(out=sel[:, 0, :], in0=sel[:, 0, :], in1=ps["e0"][:], op=ALU.add)
-                nc.vector.scalar_tensor_tensor(out=t36[:], in0=xk, scalar=1.0, in1=ps["d36"][:], op0=ALU.is_ge, op1=ALU.mult)
-                nc.vector.scalar_tensor_tensor(out=sel[:, 1, :], in0=xk, scalar=-1.0 / 3.0, in1=ps["d14"][:], op0=ALU.is_ge, op1=ALU.mult)
-                nc.vector.tensor_tensor(out=sel[:, 1, :], in0=sel[:, 1, :], in1=ps["e1"][:], op=ALU.add)
-                nc.vector.scalar_tensor_tensor(out=sel[:, 2, :], in0=xk, scalar=1.0 / 3.0, in1=ps["d25"][:], op0=ALU.is_ge, op1=ALU.mult)
-                nc.vector.tensor_tensor(out=sel[:, 2, :], in0=sel[:, 2, :], in1=ps["e2"][:], op=ALU.add)
-                nc.vector.tensor_tensor(out=sel[:, 0, :], in0=sel[:, 0, :], in1=t36[:], op=ALU.add)
-                nc.vector.tensor_tensor(out=prod[:, 0:3, :], in0=sel[:], in1=f[:], op=ALU.mult)
-                half = tp.tile([P, 2, HALF], F32, name="half", tag="half")
-                nc.vector.tensor_tensor(out=half[:], in0=prod[:, 0:2, :], in1=prod[:, 2:4, :], op=ALU.add)
-                res = tp.tile([P, HALF], F32, name="res", tag="res")
-                nc.vector.tensor_tensor(out=res[:], in0=half[:, 0, :], in1=half[:, 1, :], op=ALU.add)
-                nc.sync.dma_start(out=ov[:, k, cols], in_=res[:])
+            for k in range(NBLK):
+                pair = (2 * k, 2 * k + 1)
+                st = []
+                for i in pair:
+                    if i + AHEAD < NT:
+                        factor(i + AHEAD)
+                    st.append(sums_and_select(tp, i))
+                for sel, t36 in st:
+                    nc.vector.tensor_tensor(out=sel[:, 0, :], in0=sel[:, 0, :], in1=t36[:], op=ALU.add)
+                for (sel, t36), i in zip(st, pair):
+                    nc.vector.tensor_tensor(out=sel[:, 0:3, :], in0=sel[:, 0:3, :], in1=ftiles[i][:], op=ALU.mult)
+                for sel, t36 in st:
+                    nc.vector.tensor_tensor(out=sel[:, 0:2, :], in0=sel[:, 0:2, :], in1=sel[:, 2:4, :], op=ALU.add)
+                for (sel, t36), i in zip(st, pair):
+                    res = tp.tile([P, HALF], F32, name="res", tag="res")
+                    nc.vector.tensor_tensor(out=res[:], in0=sel[:, 0, :], in1=sel[:, 1, :], op=ALU.add)
+                    nc.sync.dma_start(out=ov[:, k, (i % 2) * HALF:(i % 2 + 1) * HALF], in_=res[:])

@@ -21,11 +21,11 @@ NB = 6
 HALF = 512
 CH = 256
 NT = 16
-AHEAD = 3
+AHEAD = 2
 PIN = False
 SUB_ON_G = True
 CLAMP_ON_G = False
-S_CHUNKS = (0,)
+S_CHUNKS = (1,)
 
 FLOPS = 2 * 1024 * 512 * 7168
 
@@ -55,8 +55,8 @@ def tile_kanoriginal_t_kernel(tc, x, coef, scale_base, scale_sp, bias, grad_out,
         if PIN:
             ctx.enter_context(tc.manual_schedule())
         keep = ctx.enter_context(tc.tile_pool(name="keep", bufs=1))
-        facw = ctx.enter_context(tc.tile_pool(name="facw", bufs=3))
-        facf = ctx.enter_context(tc.tile_pool(name="facf", bufs=AHEAD + 2))
+        facw = ctx.enter_context(tc.tile_pool(name="facw", bufs=2))
+        facf = ctx.enter_context(tc.tile_pool(name="facf", bufs=2))
         psum = ctx.enter_context(tc.psum_pool(name="psum", bufs=1))
 
         x_all = keep.tile([P, NBLK, D], BF16)
@@ -145,44 +145,64 @@ def tile_kanoriginal_t_kernel(tc, x, coef, scale_base, scale_sp, bias, grad_out,
         for k in range(NBLK):
             nc.scalar.activation(out=ds_all[:, k, :], in_=x_all[:, k, :], func=ACT.Silu, scale=-1.0)
         for k in range(NBLK):
-            sgt = facw.tile([P, 3, HALF], F32, name="sgt", tag="w")
-            sg = sgt[:].rearrange("p a b -> p (a b)")[:, 0:D]
+            sgt = facw.tile([P, 3, D], F32, name="sgt", tag="w")
+            sg = sgt[:, 0, :]
             nc.scalar.activation(out=sg, in_=x_all[:, k, :], func=ACT.Sigmoid)
             nc.vector.scalar_tensor_tensor(out=ds_all[:, k, :], in0=ds_all[:, k, :], scalar=1.0, in1=sg, op0=ALU.subtract, op1=ALU.mult)
 
-        wtiles = {}
-        ftiles = {}
+        wt = {}
+        ft = {}
+        late = {}
 
         def xslice(i):
             return x_all[:, i // 2, (i % 2) * HALF:(i % 2 + 1) * HALF]
 
-        def clamps(i):
-            xk = xslice(i)
-            xc0 = facw.tile([P, HALF], BF16, name="xc0", tag="xc0")
+        def clamps(k):
+            xk = x_all[:, k, :]
+            third = k % 3 == 2
+            xc0 = (late["w"] if third else facw).tile([P, D], BF16, name="xc0", tag="xc0")
             nc.vector.tensor_scalar(out=xc0[:], in0=xk, scalar1=3.0, scalar2=-3.0, op0=ALU.min, op1=ALU.max)
-            w = facw.tile([P, 3, HALF], F32, name="w", tag="w")
+            w = (late["w"] if third else facw).tile([P, 3, D], F32, name="w", tag="w")
             eng = nc.gpsimd if CLAMP_ON_G else nc.vector
             eng.tensor_scalar(out=w[:, 1, :], in0=xk, scalar1=5.0 / 3.0, scalar2=-7.0 / 3.0, op0=ALU.min, op1=ALU.max)
             eng.tensor_scalar(out=w[:, 2, :], in0=xk, scalar1=7.0 / 3.0, scalar2=-5.0 / 3.0, op0=ALU.min, op1=ALU.max)
-            wtiles[i] = (xc0, w)
+            wt[k] = (xc0, w)
 
-        def factor(i):
-            if i + 1 < NT:
-                clamps(i + 1)
-            xc0, w = wtiles[i]
-            nc.scalar.activation(out=w[:, 0, :], in_=xc0[:], func=ACT.Abs, scale=1.5)
-            nc.scalar.activation(out=w[:, 0, :], in_=w[:, 0, :], func=ACT.Abs, bias=-1.5)
-            nc.scalar.activation(out=w[:, 1, :], in_=w[:, 1, :], func=ACT.Abs, scale=1.5, bias=0.5)
-            nc.scalar.activation(out=w[:, 2, :], in_=w[:, 2, :], func=ACT.Abs, scale=1.5, bias=-0.5)
-            nc.scalar.activation(out=w[:], in_=w[:], func=ACT.Abs, bias=-1.5)
-            f = facf.tile([P, 3, HALF], F32, name="f", tag="f")
+        def head_ops(k):
+            if k >= NBLK:
+                return [None] * 4
+            xc0, w = wt[k]
+            act = nc.scalar.activation
+            return [
+                lambda: act(out=w[:, 0, :], in_=xc0[:], func=ACT.Abs, scale=1.5),
+                lambda: act(out=w[:, 1, :], in_=w[:, 1, :], func=ACT.Abs, scale=1.5, bias=0.5),
+                lambda: act(out=w[:, 0, :], in_=w[:, 0, :], func=ACT.Abs, bias=-1.5),
+                lambda: act(out=w[:, 2, :], in_=w[:, 2, :], func=ACT.Abs, scale=1.5, bias=-0.5),
+            ]
+
+        def factor(k):
+            if k + 1 < NBLK:
+                clamps(k + 1)
+            nxt = head_ops(k + 1)
+            xc0, w = wt[k]
+            f = (late["f"] if k % 3 == 2 else facf).tile([P, 3, D], F32, name="f", tag="f")
             r = math.sqrt(0.75)
-            nc.scalar.activation(out=f[:], in_=w[:], func=ACT.Square, scale=-r, bias=1.5 * r)
-            nc.scalar.activation(out=w[:], in_=w[:], func=ACT.Relu, scale=-1.0, bias=0.5)
-            nc.scalar.activation(out=w[:], in_=w[:], func=ACT.Square, scale=1.5)
+            act = nc.scalar.activation
+            wide = [
+                lambda: act(out=w[:], in_=w[:], func=ACT.Abs, bias=-1.5),
+                lambda: act(out=f[:], in_=w[:], func=ACT.Square, scale=-r, bias=1.5 * r),
+                lambda: act(out=w[:], in_=w[:], func=ACT.Relu, scale=-1.0, bias=0.5),
+                lambda: act(out=w[:], in_=w[:], func=ACT.Square, scale=1.5),
+            ]
+            for a, b in zip(wide, nxt):
+                a()
+                if b is not None:
+                    b()
             eng = nc.gpsimd if SUB_ON_G else nc.vector
-            eng.tensor_tensor(out=f[:], in0=f[:], in1=w[:], op=ALU.subtract)
-            ftiles[i] = f
+            for h in range(2):
+                cs = slice(h * HALF, (h + 1) * HALF)
+                eng.tensor_tensor(out=f[:, :, cs], in0=f[:, :, cs], in1=w[:, :, cs], op=ALU.subtract)
+            ft[k] = f
 
         def sums_and_select(tp, i):
             k = i // 2
@@ -217,21 +237,24 @@ def tile_kanoriginal_t_kernel(tc, x, coef, scale_base, scale_sp, bias, grad_out,
             nc.vector.tensor_tensor(out=sel[:, 3, :], in0=ds_all[:, k, cols], in1=ps["base"][:], op=ALU.mult)
             return sel, t36
 
-        with tc.tile_pool(name="tside", bufs=4) as tp:
+        with tc.tile_pool(name="tside", bufs=4) as tp, tc.tile_pool(name="latew", bufs=1) as latew, tc.tile_pool(name="latef", bufs=1) as latef:
+            late["w"] = latew
+            late["f"] = latef
             clamps(0)
-            for i in range(AHEAD):
-                factor(i)
+            for op in head_ops(0):
+                op()
+            for k in range(AHEAD):
+                factor(k)
             for k in range(NBLK):
+                if k + AHEAD < NBLK:
+                    factor(k + AHEAD)
                 pair = (2 * k, 2 * k + 1)
-                st = []
-                for i in pair:
-                    if i + AHEAD < NT:
-                        factor(i + AHEAD)
-                    st.append(sums_and_select(tp, i))
+                st = [sums_and_select(tp, i) for i in pair]
                 for sel, t36 in st:
                     nc.vector.tensor_tensor(out=sel[:, 0, :], in0=sel[:, 0, :], in1=t36[:], op=ALU.add)
                 for (sel, t36), i in zip(st, pair):
-                    nc.vector.tensor_tensor(out=sel[:, 0:3, :], in0=sel[:, 0:3, :], in1=ftiles[i][:], op=ALU.mult)
+                    cs = slice((i % 2) * HALF, (i % 2 + 1) * HALF)
+                    nc.vector.tensor_tensor(out=sel[:, 0:3, :], in0=sel[:, 0:3, :], in1=ft[k][:, :, cs], op=ALU.mult)
                 for sel, t36 in st:
                     nc.vector.tensor_tensor(out=sel[:, 0:2, :], in0=sel[:, 0:2, :], in1=sel[:, 2:4, :], op=ALU.add)
                 for (sel, t36), i in zip(st, pair):

@@ -24,8 +24,9 @@ NT = 16
 AHEAD = 2
 PIN = False
 SUB_ON_G = True
-CLAMP_ON_G = False
-S_CHUNKS = (1,)
+CLAMP_ON_G = True
+S_CHUNKS = (3,)
+GCOPY_ON_S = True
 
 FLOPS = 2 * 1024 * 512 * 7168
 
@@ -57,6 +58,7 @@ def tile_kanoriginal_t_kernel(tc, x, coef, scale_base, scale_sp, bias, grad_out,
         keep = ctx.enter_context(tc.tile_pool(name="keep", bufs=1))
         facw = ctx.enter_context(tc.tile_pool(name="facw", bufs=2))
         facf = ctx.enter_context(tc.tile_pool(name="facf", bufs=2))
+        sgp = ctx.enter_context(tc.tile_pool(name="sgp", bufs=2))
         psum = ctx.enter_context(tc.psum_pool(name="psum", bufs=1))
 
         x_all = keep.tile([P, NBLK, D], BF16)
@@ -73,18 +75,21 @@ def tile_kanoriginal_t_kernel(tc, x, coef, scale_base, scale_sp, bias, grad_out,
             eng_copy(out=dst.rearrange("p (c i) t -> p c t i", i=4), in_=src.rearrange("p t (c i) -> p c t i", i=4))
 
         with tc.tile_pool(name="prep1", bufs=1) as prep1, tc.tile_pool(name="prep2", bufs=2) as prep2:
-            g_raw = prep1.tile([P, NBLK, O], BF16, tag="ga", align_bytes=64)
-            nc.sync.dma_start(out=g_raw[:], in_=gv)
-            sp_raw = prep1.tile([P, 4, D], BF16, tag="sp")
-            nc.sync.dma_start(out=sp_raw[:], in_=spv)
+            sp_raw = prep1.tile([P, 4, D], BF16, tag="ga", align_bytes=64)
             craws = []
             for c in range(2):
                 craw = prep2.tile([P, 4, CW], BF16, name="craw%d" % c, tag="craw")
-                nc.sync.dma_start(out=craw[:], in_=cv[:, :, c * CW:(c + 1) * CW])
                 craws.append(craw)
+            nc.sync.dma_start(out=craws[0][:], in_=cv[:, :, 0:CW])
+            nc.sync.dma_start(out=sp_raw[:], in_=spv)
             nc.sync.dma_start(out=x_all[:], in_=xv)
+            nc.sync.dma_start(out=craws[1][:], in_=cv[:, :, CW:2 * CW])
 
             make_identity(nc, ident[:])
+            spg = prep1.tile([P, D, 4], BF16, tag="gc", align_bytes=64)
+            regroup(nc.vector.tensor_copy, spg[:], sp_raw[:])
+            g_raw = prep1.tile([P, NBLK, O], BF16, tag="ga", align_bytes=64)
+            nc.sync.dma_start(out=g_raw[:], in_=gv)
 
             g_pos = prep1.tile([P, NBLK * P, 4], BF16, tag="gb", align_bytes=64)
             g_pos32 = g_pos[:].rearrange("p n t -> p (n t)").bitcast(F32).rearrange("p (k n u) -> p k n u", k=NBLK, u=2)
@@ -95,18 +100,13 @@ def tile_kanoriginal_t_kernel(tc, x, coef, scale_base, scale_sp, bias, grad_out,
                     words = g_raw[:, 2 * q + kl, :].bitcast(F32).rearrange("p (w u) -> p u w", u=2)
                     for u in range(2):
                         nc.tensor.transpose(pt[:, 2 * kl + u, :], words[:, u, :], ident[:])
-                nc.vector.tensor_copy(
+                (nc.scalar.copy if GCOPY_ON_S else nc.vector.tensor_copy)(
                     out=g_pos32[:, 2 * q:2 * q + 2],
                     in_=pt[:].rearrange("p (k u) n -> p k n u", u=2),
                 )
             g_flat = g_pos[:].rearrange("p n t -> p (n t)")
-            spg = prep1.tile([P, D, 4], BF16, tag="ga", align_bytes=64)
-            regroup(nc.vector.tensor_copy, spg[:], sp_raw[:])
             nc.vector.quantize_mx(out=gq_pos[:].bitcast(E5X4), scales=gs_pos[:], in_=g_flat)
             nc.vector.tensor_scalar(out=g_flat, in0=g_flat, scalar1=-1.0, scalar2=None, op0=ALU.mult)
-
-            sb_raw = prep1.tile([P, 4, D], BF16, tag="sp")
-            nc.sync.dma_start(out=sb_raw[:], in_=sbv)
 
             neg_done = False
             for c in range(4):
@@ -136,19 +136,16 @@ def tile_kanoriginal_t_kernel(tc, x, coef, scale_base, scale_sp, bias, grad_out,
                             scales=ws[:, term, cols],
                             in_=gws[hb][:, j].rearrange("p i t -> p (i t)"),
                         )
-                if c == 1:
+                if c == 2:
+                    sb_raw = prep1.tile([P, 4, D], BF16, tag="ga", align_bytes=64)
+                    nc.sync.dma_start(out=sb_raw[:], in_=sbv)
                     sb_grp = prep1.tile([P, D, 4], BF16, tag="gb", align_bytes=64)
                     regroup(nc.scalar.copy, sb_grp[:], sb_raw[:])
-                if c == 2:
+                if c == 3:
                     nc.vector.quantize_mx(out=wq[:, 0, :].bitcast(E4X4), scales=ws[:, 0, :], in_=sb_grp[:].rearrange("p i t -> p (i t)"))
 
         for k in range(NBLK):
             nc.scalar.activation(out=ds_all[:, k, :], in_=x_all[:, k, :], func=ACT.Silu, scale=-1.0)
-        for k in range(NBLK):
-            sgt = facw.tile([P, 3, D], F32, name="sgt", tag="w")
-            sg = sgt[:, 0, :]
-            nc.scalar.activation(out=sg, in_=x_all[:, k, :], func=ACT.Sigmoid)
-            nc.vector.scalar_tensor_tensor(out=ds_all[:, k, :], in0=ds_all[:, k, :], scalar=1.0, in1=sg, op0=ALU.subtract, op1=ALU.mult)
 
         wt = {}
         ft = {}
@@ -180,7 +177,13 @@ def tile_kanoriginal_t_kernel(tc, x, coef, scale_base, scale_sp, bias, grad_out,
                 lambda: act(out=w[:, 2, :], in_=w[:, 2, :], func=ACT.Abs, scale=1.5, bias=-0.5),
             ]
 
+        def dsilu(k):
+            sg = sgp.tile([P, D], F32, name="sg", tag="sg")
+            nc.scalar.activation(out=sg[:], in_=x_all[:, k, :], func=ACT.Sigmoid)
+            nc.vector.scalar_tensor_tensor(out=ds_all[:, k, :], in0=ds_all[:, k, :], scalar=1.0, in1=sg[:], op0=ALU.subtract, op1=ALU.mult)
+
         def factor(k):
+            dsilu(k)
             if k + 1 < NBLK:
                 clamps(k + 1)
             nxt = head_ops(k + 1)

@@ -24,7 +24,7 @@ NT = 16
 AHEAD = 2
 PIN = False
 SUB_ON_G = True
-CLAMP_ON_G = True
+CLAMP_ON_G = False
 S_CHUNKS = (3,)
 GCOPY_ON_S = True
 

@@ -204,7 +204,8 @@ def tile_kanoriginal_t_kernel(tc, x, coef, scale_base, scale_sp, bias, grad_out,
             eng = nc.gpsimd if SUB_ON_G else nc.vector
             for h in range(2):
                 cs = slice(h * HALF, (h + 1) * HALF)
-                eng.tensor_tensor(out=f[:, :, cs], in0=f[:, :, cs], in1=w[:, :, cs], op=ALU.subtract)
+                for g in range(3):
+                    eng.tensor_tensor(out=f[:, g, cs], in0=f[:, g, cs], in1=w[:, g, cs], op=ALU.subtract)
             ft[k] = f
 
         def sums_and_select(tp, i):

@@ -82,7 +82,8 @@ def tile_kanoriginal_t_kernel(tc, x, coef, scale_base, scale_sp, bias, grad_out,
                 craws.append(craw)
             nc.sync.dma_start(out=craws[0][:], in_=cv[:, :, 0:CW])
             nc.sync.dma_start(out=sp_raw[:], in_=spv)
-            nc.sync.dma_start(out=x_all[:], in_=xv)
+            nc.sync.dma_start(out=x_all[:, 0:4, :], in_=xv[:, 0:4, :])
+            nc.sync.dma_start(out=x_all[:, 4:8, :], in_=xv[:, 4:8, :])
             nc.sync.dma_start(out=craws[1][:], in_=cv[:, :, CW:2 * CW])
 
             make_identity(nc, ident[:])
@@ -144,8 +145,8 @@ def tile_kanoriginal_t_kernel(tc, x, coef, scale_base, scale_sp, bias, grad_out,
                 if c == 3:
                     nc.vector.quantize_mx(out=wq[:, 0, :].bitcast(E4X4), scales=ws[:, 0, :], in_=sb_grp[:].rearrange("p i t -> p (i t)"))
 
-        for k in range(NBLK):
-            nc.scalar.activation(out=ds_all[:, k, :], in_=x_all[:, k, :], func=ACT.Silu, scale=-1.0)
+        for lo in (0, 4):
+            nc.scalar.activation(out=ds_all[:, lo:lo + 4, :], in_=x_all[:, lo:lo + 4, :], func=ACT.Silu, scale=-1.0)
 
         wt = {}
         ft = {}
@@ -167,7 +168,7 @@ def tile_kanoriginal_t_kernel(tc, x, coef, scale_base, scale_sp, bias, grad_out,
 
         def head_ops(k):
             if k >= NBLK:
-                return [None] * 4
+                return []
             xc0, w = wt[k]
             act = nc.scalar.activation
             return [
@@ -191,21 +192,31 @@ def tile_kanoriginal_t_kernel(tc, x, coef, scale_base, scale_sp, bias, grad_out,
             f = (late["f"] if k % 3 == 2 else facf).tile([P, 3, D], F32, name="f", tag="f")
             r = math.sqrt(0.75)
             act = nc.scalar.activation
-            wide = [
-                lambda: act(out=w[:], in_=w[:], func=ACT.Abs, bias=-1.5),
-                lambda: act(out=f[:], in_=w[:], func=ACT.Square, scale=-r, bias=1.5 * r),
-                lambda: act(out=w[:], in_=w[:], func=ACT.Relu, scale=-1.0, bias=0.5),
-                lambda: act(out=w[:], in_=w[:], func=ACT.Square, scale=1.5),
-            ]
-            for a, b in zip(wide, nxt):
-                a()
-                if b is not None:
-                    b()
-            eng = nc.gpsimd if SUB_ON_G else nc.vector
-            for h in range(2):
+
+            def wide_ops(cs):
+                return [
+                    lambda: act(out=w[:, :, cs], in_=w[:, :, cs], func=ACT.Abs, bias=-1.5),
+                    lambda: act(out=f[:, :, cs], in_=w[:, :, cs], func=ACT.Square, scale=-r, bias=1.5 * r),
+                    lambda: act(out=w[:, :, cs], in_=w[:, :, cs], func=ACT.Relu, scale=-1.0, bias=0.5),
+                    lambda: act(out=w[:, :, cs], in_=w[:, :, cs], func=ACT.Square, scale=1.5),
+                ]
+
+            def subtract(h):
                 cs = slice(h * HALF, (h + 1) * HALF)
                 for g in range(3):
-                    eng.tensor_tensor(out=f[:, g, cs], in0=f[:, g, cs], in1=w[:, g, cs], op=ALU.subtract)
+                    nc.gpsimd.tensor_tensor(out=f[:, g, cs], in0=f[:, g, cs], in1=w[:, g, cs], op=ALU.subtract)
+
+            if k == NBLK - 1:
+                for h in range(2):
+                    for a in wide_ops(slice(h * HALF, (h + 1) * HALF)):
+                        a()
+                    subtract(h)
+            else:
+                for a, b in zip(wide_ops(slice(0, D)), nxt):
+                    a()
+                    b()
+                subtract(0)
+                subtract(1)
             ft[k] = f
 
         def sums_and_select(tp, i):
@@ -241,6 +252,22 @@ def tile_kanoriginal_t_kernel(tc, x, coef, scale_base, scale_sp, bias, grad_out,
             nc.vector.tensor_tensor(out=sel[:, 3, :], in0=ds_all[:, k, cols], in1=ps["base"][:], op=ALU.mult)
             return sel, t36
 
+        def finish_ops(tp, sel, t36, f, i):
+            cs = slice((i % 2) * HALF, (i % 2 + 1) * HALF)
+            tt = nc.vector.tensor_tensor
+
+            def last():
+                res = tp.tile([P, HALF], F32, name="res", tag="res")
+                tt(out=res[:], in0=sel[:, 0, :], in1=sel[:, 1, :], op=ALU.add)
+                nc.sync.dma_start(out=ov[:, i // 2, cs], in_=res[:])
+
+            return [
+                lambda: tt(out=sel[:, 0, :], in0=sel[:, 0, :], in1=t36[:], op=ALU.add),
+                lambda: tt(out=sel[:, 0:3, :], in0=sel[:, 0:3, :], in1=f[:, :, cs], op=ALU.mult),
+                lambda: tt(out=sel[:, 0:2, :], in0=sel[:, 0:2, :], in1=sel[:, 2:4, :], op=ALU.add),
+                last,
+            ]
+
         with tc.tile_pool(name="tside", bufs=4) as tp, tc.tile_pool(name="latew", bufs=1) as latew, tc.tile_pool(name="latef", bufs=1) as latef:
             late["w"] = latew
             late["f"] = latef
@@ -254,14 +281,10 @@ def tile_kanoriginal_t_kernel(tc, x, coef, scale_base, scale_sp, bias, grad_out,
                     factor(k + AHEAD)
                 pair = (2 * k, 2 * k + 1)
                 st = [sums_and_select(tp, i) for i in pair]
-                for sel, t36 in st:
-                    nc.vector.tensor_tensor(out=sel[:, 0, :], in0=sel[:, 0, :], in1=t36[:], op=ALU.add)
-                for (sel, t36), i in zip(st, pair):
-                    cs = slice((i % 2) * HALF, (i % 2 + 1) * HALF)
-                    nc.vector.tensor_tensor(out=sel[:, 0:3, :], in0=sel[:, 0:3, :], in1=ft[k][:, :, cs], op=ALU.mult)
-                for sel, t36 in st:
-                    nc.vector.tensor_tensor(out=sel[:, 0:2, :], in0=sel[:, 0:2, :], in1=sel[:, 2:4, :], op=ALU.add)
-                for (sel, t36), i in zip(st, pair):
-                    res = tp.tile([P, HALF], F32, name="res", tag="res")
-                    nc.vector.tensor_tensor(out=res[:], in0=sel[:, 0, :], in1=sel[:, 1, :], op=ALU.add)
-                    nc.sync.dma_start(out=ov[:, k, (i % 2) * HALF:(i % 2 + 1) * HALF], in_=res[:])
+                steps = [finish_ops(tp, sel, t36, ft[k], i) for (sel, t36), i in zip(st, pair)]
+                if k == NBLK - 1:
+                    order = steps[0] + steps[1]
+                else:
+                    order = [op for both in zip(steps[0], steps[1]) for op in both]
+                for op in order:
+                    op()

from contextlib import ExitStack
import math

import concourse.mybir as mybir
from concourse.masks import make_identity

F32 = mybir.dt.float32
BF16 = mybir.dt.bfloat16
U32 = mybir.dt.uint32
U8 = mybir.dt.uint8
E4X4 = mybir.dt.float8_e4m3fn_x4
E5X4 = mybir.dt.float8_e5m2_x4
ALU = mybir.AluOpType
ACT = mybir.ActivationFunctionType

P = 128
NBLK = 8
D = 1024
O = 512
NB = 6
HALF = 512
CH = 256
NT = 16
AHEAD = 2
PIN = False
SUB_ON_G = True
CLAMP_ON_G = False
S_CHUNKS = (3,)
GCOPY_ON_S = True

FLOPS = 2 * 1024 * 512 * 7168

SUMS = (
    ("d03", ((1, 4), (-1, 3), (-1, 1))),
    ("d14", ((1, 5), (-1, 4), (-1, 2), (1, 1))),
    ("d25", ((1, 6), (-1, 5), (-1, 3), (1, 2))),
    ("d36", ((-1, 6), (-1, 4), (1, 3))),
    ("e0", ((1, 1),)),
    ("e1", ((1, 2), (-1, 1))),
    ("e2", ((1, 3), (-1, 2))),
    ("base", ((-1, 0),)),
)


def tile_kanoriginal_t_kernel(tc, x, coef, scale_base, scale_sp, bias, grad_out, out):
    nc = tc.nc
    xv = x.flatten_outer_dims().rearrange("(p k) d -> p k d", k=NBLK)
    gv = grad_out.flatten_outer_dims().rearrange("(p k) o -> p k o", k=NBLK)
    ov = out.flatten_outer_dims().rearrange("(p k) d -> p k d", k=NBLK)
    cv = coef.rearrange("(p t) i b -> p t (i b)", t=4)
    spv = scale_sp.rearrange("(p t) i -> p t i", t=4)
    sbv = scale_base.rearrange("(p t) i -> p t i", t=4)
    CW = CH * NB

    with ExitStack() as ctx:
        if PIN:
            ctx.enter_context(tc.manual_schedule())
        keep = ctx.enter_context(tc.tile_pool(name="keep", bufs=1))
        facw = ctx.enter_context(tc.tile_pool(name="facw", bufs=2))
        facf = ctx.enter_context(tc.tile_pool(name="facf", bufs=2))
        sgp = ctx.enter_context(tc.tile_pool(name="sgp", bufs=2))
        psum = ctx.enter_context(tc.psum_pool(name="psum", bufs=1))

        x_all = keep.tile([P, NBLK, D], BF16)
        ds_all = keep.tile([P, NBLK, D], F32)
        wq = keep.tile([P, 7, D], U32, align_bytes=64)
        ws = keep.tile([P, 7, D], U8, align_bytes=64)
        gq_pos = keep.tile([P, NBLK * P], U32, align_bytes=64)
        gs_pos = keep.tile([P, NBLK * P], U8, align_bytes=64)
        gq_neg = keep.tile([P, NBLK * P], U32, align_bytes=64)
        gs_neg = keep.tile([P, NBLK * P], U8, align_bytes=64)
        ident = keep.tile([P, P], F32)

        def regroup(eng_copy, dst, src):
            eng_copy(out=dst.rearrange("p (c i) t -> p c t i", i=4), in_=src.rearrange("p t (c i) -> p c t i", i=4))

        with tc.tile_pool(name="prep1", bufs=1) as prep1, tc.tile_pool(name="prep2", bufs=2) as prep2:
            sp_raw = prep1.tile([P, 4, D], BF16, tag="ga", align_bytes=64)
            craws = []
            for c in range(2):
                craw = prep2.tile([P, 4, CW], BF16, name="craw%d" % c, tag="craw")
                craws.append(craw)
            nc.sync.dma_start(out=craws[0][:], in_=cv[:, :, 0:CW])
            nc.sync.dma_start(out=sp_raw[:], in_=spv)
            nc.sync.dma_start(out=x_all[:, 0:4, :], in_=xv[:, 0:4, :])
            nc.sync.dma_start(out=x_all[:, 4:8, :], in_=xv[:, 4:8, :])
            nc.sync.dma_start(out=craws[1][:], in_=cv[:, :, CW:2 * CW])

            make_identity(nc, ident[:])
            spg = prep1.tile([P, D, 4], BF16, tag="gc", align_bytes=64)
            regroup(nc.vector.tensor_copy, spg[:], sp_raw[:])
            g_raw = prep1.tile([P, NBLK, O], BF16, tag="ga", align_bytes=64)
            nc.sync.dma_start(out=g_raw[:], in_=gv)

            g_pos = prep1.tile([P, NBLK * P, 4], BF16, tag="gb", align_bytes=64)
            g_pos32 = g_pos[:].rearrange("p n t -> p (n t)").bitcast(F32).rearrange("p (k n u) -> p k n u", k=NBLK, u=2)
            names = [s[0] for s in SUMS]
            for q in range(4):
                pt = psum.tile([P, 4, P], F32, name="pt%d" % q, tag=names[q])
                for kl in range(2):
                    words = g_raw[:, 2 * q + kl, :].bitcast(F32).rearrange("p (w u) -> p u w", u=2)
                    for u in range(2):
                        nc.tensor.transpose(pt[:, 2 * kl + u, :], words[:, u, :], ident[:])
                (nc.scalar.copy if GCOPY_ON_S else nc.vector.tensor_copy)(
                    out=g_pos32[:, 2 * q:2 * q + 2],
                    in_=pt[:].rearrange("p (k u) n -> p k n u", u=2),
                )
            g_flat = g_pos[:].rearrange("p n t -> p (n t)")
            nc.vector.quantize_mx(out=gq_pos[:].bitcast(E5X4), scales=gs_pos[:], in_=g_flat)
            nc.vector.tensor_scalar(out=g_flat, in0=g_flat, scalar1=-1.0, scalar2=None, op0=ALU.mult)

            neg_done = False
            for c in range(4):
                if c < 2:
                    craw = craws[c]
                else:
                    craw = prep2.tile([P, 4, CW], BF16, name="craw%d" % c, tag="craw")
                    nc.sync.dma_start(out=craw[:], in_=cv[:, :, c * CW:(c + 1) * CW])
                cols = slice(c * CH, (c + 1) * CH)
                cg = prep2.tile([P, CW, 4], BF16, name="cg", tag="cg")
                regroup(nc.scalar.copy if c in S_CHUNKS else nc.vector.tensor_copy, cg[:], craw[:])
                if not neg_done:
                    nc.vector.quantize_mx(out=gq_neg[:].bitcast(E5X4), scales=gs_neg[:], in_=g_flat)
                    neg_done = True
                cview = cg[:].rearrange("p (i b) t -> p b i t", b=NB)
                sview = spg[:, cols, :].unsqueeze(1).to_broadcast([P, 3, CH, 4])
                gws = []
                for hb in range(2):
                    gw = prep2.tile([P, 3, CH, 4], BF16, name="gw%d" % hb, tag="gw", align_bytes=64)
                    nc.vector.tensor_tensor(out=gw[:], in0=cview[:, 3 * hb:3 * hb + 3], in1=sview, op=ALU.mult)
                    gws.append(gw)
                for hb in range(2):
                    for j in range(3):
                        term = 1 + 3 * hb + j
                        nc.vector.quantize_mx(
                            out=wq[:, term, cols].bitcast(E4X4),
                            scales=ws[:, term, cols],
                            in_=gws[hb][:, j].rearrange("p i t -> p (i t)"),
                        )
                if c == 2:
                    sb_raw = prep1.tile([P, 4, D], BF16, tag="ga", align_bytes=64)
                    nc.sync.dma_start(out=sb_raw[:], in_=sbv)
                    sb_grp = prep1.tile([P, D, 4], BF16, tag="gb", align_bytes=64)
                    regroup(nc.scalar.copy, sb_grp[:], sb_raw[:])
                if c == 3:
                    nc.vector.quantize_mx(out=wq[:, 0, :].bitcast(E4X4), scales=ws[:, 0, :], in_=sb_grp[:].rearrange("p i t -> p (i t)"))

        for lo in (0, 4):
            nc.scalar.activation(out=ds_all[:, lo:lo + 4, :], in_=x_all[:, lo:lo + 4, :], func=ACT.Silu, scale=-1.0)

        wt = {}
        ft = {}
        late = {}

        def xslice(i):
            return x_all[:, i // 2, (i % 2) * HALF:(i % 2 + 1) * HALF]

        def clamps(k):
            xk = x_all[:, k, :]
            third = k % 3 == 2
            xc0 = (late["w"] if third else facw).tile([P, D], BF16, name="xc0", tag="xc0")
            nc.vector.tensor_scalar(out=xc0[:], in0=xk, scalar1=3.0, scalar2=-3.0, op0=ALU.min, op1=ALU.max)
            w = (late["w"] if third else facw).tile([P, 3, D], F32, name="w", tag="w")
            eng = nc.gpsimd if CLAMP_ON_G else nc.vector
            eng.tensor_scalar(out=w[:, 1, :], in0=xk, scalar1=5.0 / 3.0, scalar2=-7.0 / 3.0, op0=ALU.min, op1=ALU.max)
            eng.tensor_scalar(out=w[:, 2, :], in0=xk, scalar1=7.0 / 3.0, scalar2=-5.0 / 3.0, op0=ALU.min, op1=ALU.max)
            wt[k] = (xc0, w)

        def head_ops(k):
            if k >= NBLK:
                return []
            xc0, w = wt[k]
            act = nc.scalar.activation
            return [
                lambda: act(out=w[:, 0, :], in_=xc0[:], func=ACT.Abs, scale=1.5),
                lambda: act(out=w[:, 1, :], in_=w[:, 1, :], func=ACT.Abs, scale=1.5, bias=0.5),
                lambda: act(out=w[:, 0, :], in_=w[:, 0, :], func=ACT.Abs, bias=-1.5),
                lambda: act(out=w[:, 2, :], in_=w[:, 2, :], func=ACT.Abs, scale=1.5, bias=-0.5),
            ]

        def dsilu(k):
            sg = sgp.tile([P, D], F32, name="sg", tag="sg")
            nc.scalar.activation(out=sg[:], in_=x_all[:, k, :], func=ACT.Sigmoid)
            nc.vector.scalar_tensor_tensor(out=ds_all[:, k, :], in0=ds_all[:, k, :], scalar=1.0, in1=sg[:], op0=ALU.subtract, op1=ALU.mult)

        def factor(k):
            dsilu(k)
            if k + 1 < NBLK:
                clamps(k + 1)
            nxt = head_ops(k + 1)
            xc0, w = wt[k]
            f = (late["f"] if k % 3 == 2 else facf).tile([P, 3, D], F32, name="f", tag="f")
            r = math.sqrt(0.75)
            act = nc.scalar.activation

            def wide_ops(cs):
                return [
                    lambda: act(out=w[:, :, cs], in_=w[:, :, cs], func=ACT.Abs, bias=-1.5),
                    lambda: act(out=f[:, :, cs], in_=w[:, :, cs], func=ACT.Square, scale=-r, bias=1.5 * r),
                    lambda: act(out=w[:, :, cs], in_=w[:, :, cs], func=ACT.Relu, scale=-1.0, bias=0.5),
                    lambda: act(out=w[:, :, cs], in_=w[:, :, cs], func=ACT.Square, scale=1.5),
                ]

            def subtract(h):
                cs = slice(h * HALF, (h + 1) * HALF)
                for g in range(3):
                    nc.gpsimd.tensor_tensor(out=f[:, g, cs], in0=f[:, g, cs], in1=w[:, g, cs], op=ALU.subtract)

            if k == NBLK - 1:
                for h in range(2):
                    for a in wide_ops(slice(h * HALF, (h + 1) * HALF)):
                        a()
                    subtract(h)
            else:
                for a, b in zip(wide_ops(slice(0, D)), nxt):
                    a()
                    b()
                subtract(0)
                subtract(1)
            ft[k] = f

        def sums_and_select(tp, i):
            k = i // 2
            tok = slice(k * P, (k + 1) * P)
            cols = slice((i % 2) * HALF, (i % 2 + 1) * HALF)
            ps = {}
            for name, passes in SUMS:
                acc = psum.tile([P, HALF], F32, name="ps_" + name, tag=name)
                ps[name] = acc
                for j, (sign, term) in enumerate(passes):
                    gq = gq_pos if sign > 0 else gq_neg
                    gs = gs_pos if sign > 0 else gs_neg
                    nc.tensor.matmul_mx(
                        out=acc[:],
                        lhsT=gq[:, tok].bitcast(E5X4),
                        lhsT_scale=gs[:, tok],
                        rhs=wq[:, term, cols].bitcast(E4X4),
                        rhs_scale=ws[:, term, cols],
                        start=(j == 0),
                        stop=(j == len(passes) - 1),
                    )
            xk = xslice(i)
            sel = tp.tile([P, 4, HALF], F32, name="sel", tag="sel")
            t36 = tp.tile([P, HALF], F32, name="t36", tag="t36")
            stt = nc.vector.scalar_tensor_tensor
            stt(out=sel[:, 0, :], in0=xk, scalar=-1.0, in1=ps["d03"][:], op0=ALU.is_ge, op1=ALU.mult)
            stt(out=sel[:, 1, :], in0=xk, scalar=-1.0 / 3.0, in1=ps["d14"][:], op0=ALU.is_ge, op1=ALU.mult)
            stt(out=sel[:, 2, :], in0=xk, scalar=1.0 / 3.0, in1=ps["d25"][:], op0=ALU.is_ge, op1=ALU.mult)
            stt(out=t36[:], in0=xk, scalar=1.0, in1=ps["d36"][:], op0=ALU.is_ge, op1=ALU.mult)
            for r in range(3):
                nc.vector.tensor_tensor(out=sel[:, r, :], in0=sel[:, r, :], in1=ps["e%d" % r][:], op=ALU.add)
            nc.vector.tensor_tensor(out=sel[:, 3, :], in0=ds_all[:, k, cols], in1=ps["base"][:], op=ALU.mult)
            return sel, t36

        def finish_ops(tp, sel, t36, f, i):
            cs = slice((i % 2) * HALF, (i % 2 + 1) * HALF)
            tt = nc.vector.tensor_tensor

            def last():
                res = tp.tile([P, HALF], F32, name="res", tag="res")
                tt(out=res[:], in0=sel[:, 0, :], in1=sel[:, 1, :], op=ALU.add)
                nc.sync.dma_start(out=ov[:, i // 2, cs], in_=res[:])

            return [
                lambda: tt(out=sel[:, 0, :], in0=sel[:, 0, :], in1=t36[:], op=ALU.add),
                lambda: tt(out=sel[:, 0:3, :], in0=sel[:, 0:3, :], in1=f[:, :, cs], op=ALU.mult),
                lambda: tt(out=sel[:, 0:2, :], in0=sel[:, 0:2, :], in1=sel[:, 2:4, :], op=ALU.add),
                last,
            ]

        with tc.tile_pool(name="tside", bufs=4) as tp, tc.tile_pool(name="latew", bufs=1) as latew, tc.tile_pool(name="latef", bufs=1) as latef:
            late["w"] = latew
            late["f"] = latef
            clamps(0)
            for op in head_ops(0):
                op()
            for k in range(AHEAD):
                factor(k)
            for k in range(NBLK):
                if k + AHEAD < NBLK:
                    factor(k + AHEAD)
                pair = (2 * k, 2 * k + 1)
                st = [sums_and_select(tp, i) for i in pair]
                steps = [finish_ops(tp, sel, t36, ft[k], i) for (sel, t36), i in zip(st, pair)]
                if k == NBLK - 1:
                    order = steps[0] + steps[1]
                else:
                    order = [op for both in zip(steps[0], steps[1]) for op in both]
                for op in order:
                    op()
